import numpy as np
import ml_dtypes

BF16 = ml_dtypes.bfloat16


def bf(x):
    return np.asarray(x, np.float32).astype(BF16)


def f32(x):
    return np.asarray(x, np.float32)


def f64(x):
    return np.asarray(x).astype(np.float64)


def striped(idx):
    return np.tile(idx.reshape(-1, 16).T, (8, 1))


D, S, N, P, T, K = 128, 1024, 512, 4, 128, 2
SLOPE = 0.01
WSCALE = 2.0


def leaky(v):
    return np.maximum(v, 0.0) + SLOPE * np.minimum(v, 0.0)


def layer(v, w):
    res = np.zeros((D, N))
    for p in range(P):
        acc = np.zeros((D, T))
        for r in range(K):
            e = (p + r) % P
            acc = acc + w[:, e * D:(e + 1) * D].T @ v[:, p * T:(p + 1) * T]
        res[:, p * T:(p + 1) * T] = leaky(acc / K)
    return res


def setup_inputs():
    return {"table": bf(np.random.standard_normal((D, S))), "w0": bf(WSCALE * np.random.standard_normal((D, P * D)) / np.sqrt(D)), "w1": bf(WSCALE * np.random.standard_normal((D, P * D)) / np.sqrt(D)), "offs": striped(np.random.permutation(S)[:N])}


def reference(table, w0, w1, offs):
    idx = offs[:16].T.reshape(-1)
    h = layer(f64(table)[:, idx], f64(w0))
    return layer(h, f64(w1))

@@ -1,0 +1,75 @@
+import concourse.mybir as mybir
+
+BF16, F32, U16 = mybir.dt.bfloat16, mybir.dt.float32, mybir.dt.uint16
+MULT, MAX = mybir.AluOpType.mult, mybir.AluOpType.max
+COPY = mybir.ActivationFunctionType.Copy
+
+FEATURES = 128
+SAMPLES = 1024
+PICKED = 512
+GROUPS = 4
+GROUP = PICKED // GROUPS
+EXPERTS_OF_A_GROUP = 2
+OFFSET_COLUMNS = GROUP // 16
+MEAN = 1.0 / EXPERTS_OF_A_GROUP
+SLOPE = 0.01
+
+FLOPS = 2 * (2 * FEATURES * FEATURES * PICKED * EXPERTS_OF_A_GROUP)
+BYTES = (
+    FEATURES * PICKED * 2
+    + 2 * FEATURES * GROUPS * FEATURES * 2
+    + PICKED * 2
+    + FEATURES * PICKED * 4
+)
+
+
+def mean_then_leaky(nc, pool, result, total):
+    sloped = pool.tile([FEATURES, GROUP], F32, name="sloped")
+    nc.scalar.activation(sloped[:], total, COPY, scale=MEAN * SLOPE)
+    nc.vector.scalar_tensor_tensor(result, total, MEAN, sloped[:], MULT, MAX)
+
+
+def tile_newmoe_kernel(tc, table, w0, w1, offs, out):
+    nc = tc.nc
+    with (
+        tc.tile_pool(name="held", bufs=1) as held,
+        tc.tile_pool(name="work", bufs=GROUPS) as work,
+        tc.psum_pool(name="psum", bufs=GROUPS) as psum,
+    ):
+        offsets = held.tile([FEATURES, PICKED // 16], U16, name="offsets")
+        nc.sync.dma_start(offsets[:], offs)
+        window = held.tile([FEATURES, SAMPLES], BF16, name="window")
+        nc.sync.dma_start(window[:], table)
+        experts0 = held.tile([FEATURES, GROUPS * FEATURES], BF16, name="experts0")
+        nc.scalar.dma_start(experts0[:], w0)
+        experts1 = held.tile([FEATURES, GROUPS * FEATURES], BF16, name="experts1")
+        nc.scalar.dma_start(experts1[:], w1)
+
+        for p in range(GROUPS):
+            experts_of_p = [(p + r) % GROUPS for r in range(EXPERTS_OF_A_GROUP)]
+            first, last = experts_of_p[0], experts_of_p[-1]
+
+            total0 = psum.tile([FEATURES, GROUP], F32, name="total0")
+            for e in experts_of_p:
+                nc.tensor.matmul(
+                    total0[:],
+                    experts0[:, e * FEATURES : (e + 1) * FEATURES],
+                    window[:].indirect(offsets[:, p * OFFSET_COLUMNS : (p + 1) * OFFSET_COLUMNS]),
+                    start=(e == first),
+                    stop=(e == last),
+                )
+            hidden = work.tile([FEATURES, GROUP], BF16, name="hidden")
+            mean_then_leaky(nc, work, hidden[:], total0[:])
+
+            total1 = psum.tile([FEATURES, GROUP], F32, name="total1")
+            for e in experts_of_p:
+                nc.tensor.matmul(
+                    total1[:],
+                    experts1[:, e * FEATURES : (e + 1) * FEATURES],
+                    hidden[:],
+                    start=(e == first),
+                    stop=(e == last),
+                )
+            result = work.tile([FEATURES, GROUP], F32, name="result")
+            mean_then_leaky(nc, work, result[:], total1[:])
+            nc.sync.dma_start(out[:, p * GROUP : (p + 1) * GROUP], result[:])

@@ -45,30 +45,32 @@ def tile_newmoe_kernel(tc, table, w0, w1, offs, out):
         experts1 = held.tile([FEATURES, GROUPS * FEATURES], BF16, name="experts1")
         nc.scalar.dma_start(experts1[:], w1)
 
-        for p in range(GROUPS):
-            experts_of_p = [(p + r) % GROUPS for r in range(EXPERTS_OF_A_GROUP)]
-            first, last = experts_of_p[0], experts_of_p[-1]
+        def experts_of(p):
+            return [(p + r) % GROUPS for r in range(EXPERTS_OF_A_GROUP)]
 
+        hidden = []
+        for p in range(GROUPS):
             total0 = psum.tile([FEATURES, GROUP], F32, name="total0")
-            for e in experts_of_p:
+            for r, e in enumerate(experts_of(p)):
                 nc.tensor.matmul(
                     total0[:],
                     experts0[:, e * FEATURES : (e + 1) * FEATURES],
                     window[:].indirect(offsets[:, p * OFFSET_COLUMNS : (p + 1) * OFFSET_COLUMNS]),
-                    start=(e == first),
-                    stop=(e == last),
+                    start=(r == 0),
+                    stop=(r == EXPERTS_OF_A_GROUP - 1),
                 )
-            hidden = work.tile([FEATURES, GROUP], BF16, name="hidden")
-            mean_then_leaky(nc, work, hidden[:], total0[:])
+            hidden.append(work.tile([FEATURES, GROUP], BF16, name="hidden"))
+            mean_then_leaky(nc, work, hidden[p][:], total0[:])
 
+        for p in range(GROUPS):
             total1 = psum.tile([FEATURES, GROUP], F32, name="total1")
-            for e in experts_of_p:
+            for r, e in enumerate(experts_of(p)):
                 nc.tensor.matmul(
                     total1[:],
                     experts1[:, e * FEATURES : (e + 1) * FEATURES],
-                    hidden[:],
-                    start=(e == first),
-                    stop=(e == last),
+                    hidden[p][:],
+                    start=(r == 0),
+                    stop=(r == EXPERTS_OF_A_GROUP - 1),
                 )
             result = work.tile([FEATURES, GROUP], F32, name="result")
             mean_then_leaky(nc, work, result[:], total1[:])

@@ -13,6 +13,9 @@ EXPERTS_OF_A_GROUP = 2
 OFFSET_COLUMNS = GROUP // 16
 MEAN = 1.0 / EXPERTS_OF_A_GROUP
 SLOPE = 0.01
+PSUM_BANKS = 8
+BANK = 512
+WARM_UP = 4
 
 FLOPS = 2 * (2 * FEATURES * FEATURES * PICKED * EXPERTS_OF_A_GROUP)
 BYTES = (
@@ -29,12 +32,17 @@ def mean_then_leaky(nc, pool, result, total):
     nc.vector.scalar_tensor_tensor(result, total, MEAN, sloped[:], MULT, MAX)
 
 
+def experts_of(p):
+    return [(p + r) % GROUPS for r in range(EXPERTS_OF_A_GROUP)]
+
+
 def tile_newmoe_kernel(tc, table, w0, w1, offs, out):
     nc = tc.nc
     with (
         tc.tile_pool(name="held", bufs=1) as held,
         tc.tile_pool(name="work", bufs=GROUPS) as work,
-        tc.psum_pool(name="psum", bufs=GROUPS) as psum,
+        tc.psum_pool(name="unread", bufs=1) as unread,
+        tc.psum_pool(name="psum", bufs=PSUM_BANKS - 1) as psum,
     ):
         offsets = held.tile([FEATURES, PICKED // 16], U16, name="offsets")
         nc.sync.dma_start(offsets[:], offs)
@@ -45,33 +53,36 @@ def tile_newmoe_kernel(tc, table, w0, w1, offs, out):
         experts1 = held.tile([FEATURES, GROUPS * FEATURES], BF16, name="experts1")
         nc.scalar.dma_start(experts1[:], w1)
 
-        def experts_of(p):
-            return [(p + r) % GROUPS for r in range(EXPERTS_OF_A_GROUP)]
+        zeros = held.tile([FEATURES, BANK], BF16, name="zeros")
+        nc.vector.memset(zeros[:], 0.0)
+        product = unread.tile([FEATURES, BANK], F32, name="product")
+        for i in range(WARM_UP):
+            nc.tensor.matmul(product[:], zeros[:, 0:FEATURES], zeros[:], start=True, stop=True)
 
         hidden = []
         for p in range(GROUPS):
-            total0 = psum.tile([FEATURES, GROUP], F32, name="total0")
+            total = psum.tile([FEATURES, GROUP], F32, name="total")
             for r, e in enumerate(experts_of(p)):
                 nc.tensor.matmul(
-                    total0[:],
+                    total[:],
                     experts0[:, e * FEATURES : (e + 1) * FEATURES],
                     window[:].indirect(offsets[:, p * OFFSET_COLUMNS : (p + 1) * OFFSET_COLUMNS]),
                     start=(r == 0),
                     stop=(r == EXPERTS_OF_A_GROUP - 1),
                 )
             hidden.append(work.tile([FEATURES, GROUP], BF16, name="hidden"))
-            mean_then_leaky(nc, work, hidden[p][:], total0[:])
+            mean_then_leaky(nc, work, hidden[p][:], total[:])
 
         for p in range(GROUPS):
-            total1 = psum.tile([FEATURES, GROUP], F32, name="total1")
+            total = psum.tile([FEATURES, GROUP], F32, name="total")
             for r, e in enumerate(experts_of(p)):
                 nc.tensor.matmul(
-                    total1[:],
+                    total[:],
                     experts1[:, e * FEATURES : (e + 1) * FEATURES],
                     hidden[p][:],
                     start=(r == 0),
                     stop=(r == EXPERTS_OF_A_GROUP - 1),
                 )
             result = work.tile([FEATURES, GROUP], F32, name="result")
-            mean_then_leaky(nc, work, result[:], total1[:])
+            mean_then_leaky(nc, work, result[:], total[:])
             nc.sync.dma_start(out[:, p * GROUP : (p + 1) * GROUP], result[:])

@@ -27,9 +27,9 @@ BYTES = (
 
 
 def mean_then_leaky(nc, pool, result, total):
-    sloped = pool.tile([FEATURES, GROUP], F32, name="sloped")
-    nc.scalar.activation(sloped[:], total, COPY, scale=MEAN * SLOPE)
-    nc.vector.scalar_tensor_tensor(result, total, MEAN, sloped[:], MULT, MAX)
+    mean = pool.tile([FEATURES, GROUP], F32, name="mean")
+    nc.scalar.activation(mean[:], total, COPY, scale=MEAN)
+    nc.vector.scalar_tensor_tensor(result, mean[:], SLOPE, mean[:], MULT, MAX)
 
 
 def experts_of(p):

@@ -26,21 +26,27 @@ BYTES = (
 )
 
 
-def mean_then_leaky(nc, pool, result, total):
+def mean_then_leaky(nc, pool, result, total, width):
     mean = pool.tile([FEATURES, GROUP], F32, name="mean")
-    nc.scalar.activation(mean[:], total, COPY, scale=MEAN)
-    nc.vector.scalar_tensor_tensor(result, mean[:], SLOPE, mean[:], MULT, MAX)
+    nc.scalar.activation(mean[:, 0:width], total, COPY, scale=MEAN)
+    nc.vector.scalar_tensor_tensor(result, mean[:, 0:width], SLOPE, mean[:, 0:width], MULT, MAX)
 
 
 def experts_of(p):
     return [(p + r) % GROUPS for r in range(EXPERTS_OF_A_GROUP)]
 
 
+def pieces_of(p):
+    cuts = 2 if p == GROUPS - 1 else 1
+    width = GROUP // cuts
+    return [(c * width, width) for c in range(cuts)]
+
+
 def tile_newmoe_kernel(tc, table, w0, w1, offs, out):
     nc = tc.nc
     with (
         tc.tile_pool(name="held", bufs=1) as held,
-        tc.tile_pool(name="work", bufs=GROUPS) as work,
+        tc.tile_pool(name="work", bufs=GROUPS + 1) as work,
         tc.psum_pool(name="unread", bufs=1) as unread,
         tc.psum_pool(name="psum", bufs=PSUM_BANKS - 1) as psum,
     ):
@@ -71,18 +77,22 @@ def tile_newmoe_kernel(tc, table, w0, w1, offs, out):
                     stop=(r == EXPERTS_OF_A_GROUP - 1),
                 )
             hidden.append(work.tile([FEATURES, GROUP], BF16, name="hidden"))
-            mean_then_leaky(nc, work, hidden[p][:], total[:])
+            for first, width in pieces_of(p):
+                piece = slice(first, first + width)
+                mean_then_leaky(nc, work, hidden[p][:, piece], total[:, piece], width)
 
         for p in range(GROUPS):
-            total = psum.tile([FEATURES, GROUP], F32, name="total")
-            for r, e in enumerate(experts_of(p)):
-                nc.tensor.matmul(
-                    total[:],
-                    experts1[:, e * FEATURES : (e + 1) * FEATURES],
-                    hidden[p][:],
-                    start=(r == 0),
-                    stop=(r == EXPERTS_OF_A_GROUP - 1),
-                )
             result = work.tile([FEATURES, GROUP], F32, name="result")
-            mean_then_leaky(nc, work, result[:], total[:])
+            for first, width in pieces_of(p):
+                piece = slice(first, first + width)
+                total = psum.tile([FEATURES, GROUP], F32, name="total")
+                for r, e in enumerate(experts_of(p)):
+                    nc.tensor.matmul(
+                        total[:, 0:width],
+                        experts1[:, e * FEATURES : (e + 1) * FEATURES],
+                        hidden[p][:, piece],
+                        start=(r == 0),
+                        stop=(r == EXPERTS_OF_A_GROUP - 1),
+                    )
+                mean_then_leaky(nc, work, result[:, piece], total[:, 0:width], width)
             nc.sync.dma_start(out[:, p * GROUP : (p + 1) * GROUP], result[:])

@@ -15,7 +15,7 @@ MEAN = 1.0 / EXPERTS_OF_A_GROUP
 SLOPE = 0.01
 PSUM_BANKS = 8
 BANK = 512
-WARM_UP = 4
+WARM_UP = 3
 
 FLOPS = 2 * (2 * FEATURES * FEATURES * PICKED * EXPERTS_OF_A_GROUP)
 BYTES = (
@@ -50,10 +50,10 @@ def tile_newmoe_kernel(tc, table, w0, w1, offs, out):
         tc.psum_pool(name="unread", bufs=1) as unread,
         tc.psum_pool(name="psum", bufs=PSUM_BANKS - 1) as psum,
     ):
-        offsets = held.tile([FEATURES, PICKED // 16], U16, name="offsets")
-        nc.sync.dma_start(offsets[:], offs)
         window = held.tile([FEATURES, SAMPLES], BF16, name="window")
         nc.sync.dma_start(window[:], table)
+        offsets = held.tile([FEATURES, PICKED // 16], U16, name="offsets")
+        nc.sync.dma_start(offsets[:], offs)
         experts0 = held.tile([FEATURES, GROUPS * FEATURES], BF16, name="experts0")
         nc.scalar.dma_start(experts0[:], w0)
         experts1 = held.tile([FEATURES, GROUPS * FEATURES], BF16, name="experts1")

@@ -37,7 +37,7 @@ def experts_of(p):
 
 
 def pieces_of(p):
-    cuts = 2 if p == GROUPS - 1 else 1
+    cuts = 2
     width = GROUP // cuts
     return [(c * width, width) for c in range(cuts)]
 
@@ -46,7 +46,7 @@ def tile_newmoe_kernel(tc, table, w0, w1, offs, out):
     nc = tc.nc
     with (
         tc.tile_pool(name="held", bufs=1) as held,
-        tc.tile_pool(name="work", bufs=GROUPS + 1) as work,
+        tc.tile_pool(name="work", bufs=2 * GROUPS) as work,
         tc.psum_pool(name="unread", bufs=1) as unread,
         tc.psum_pool(name="psum", bufs=PSUM_BANKS - 1) as psum,
     ):

@@ -81,8 +81,10 @@ def tile_newmoe_kernel(tc, table, w0, w1, offs, out):
                 piece = slice(first, first + width)
                 mean_then_leaky(nc, work, hidden[p][:, piece], total[:, piece], width)
 
-        for p in range(GROUPS):
-            result = work.tile([FEATURES, GROUP], F32, name="result")
+        first_two = work.tile([FEATURES, 2 * GROUP], F32, name="first_two")
+        results = [first_two[:, 0:GROUP], first_two[:, GROUP : 2 * GROUP]]
+        results += [work.tile([FEATURES, GROUP], F32, name="result")[:] for p in range(2, GROUPS)]
+        for p, result in enumerate(results):
             for first, width in pieces_of(p):
                 piece = slice(first, first + width)
                 total = psum.tile([FEATURES, GROUP], F32, name="total")
@@ -95,4 +97,7 @@ def tile_newmoe_kernel(tc, table, w0, w1, offs, out):
                         stop=(r == EXPERTS_OF_A_GROUP - 1),
                     )
                 mean_then_leaky(nc, work, result[:, piece], total[:, 0:width], width)
-            nc.sync.dma_start(out[:, p * GROUP : (p + 1) * GROUP], result[:])
+            if p == 1:
+                nc.sync.dma_start(out[:, 0 : 2 * GROUP], first_two[:])
+            elif p > 1:
+                nc.sync.dma_start(out[:, p * GROUP : (p + 1) * GROUP], result)

@@ -36,6 +36,11 @@ def experts_of(p):
     return [(p + r) % GROUPS for r in range(EXPERTS_OF_A_GROUP)]
 
 
+def expert_of(halves, e):
+    half, place = divmod(e, GROUPS // 2)
+    return halves[half][:, place * FEATURES : (place + 1) * FEATURES]
+
+
 def pieces_of(p):
     cuts = 2
     width = GROUP // cuts
@@ -54,10 +59,12 @@ def tile_newmoe_kernel(tc, table, w0, w1, offs, out):
         nc.sync.dma_start(window[:], table)
         offsets = held.tile([FEATURES, PICKED // 16], U16, name="offsets")
         nc.sync.dma_start(offsets[:], offs)
-        experts0 = held.tile([FEATURES, GROUPS * FEATURES], BF16, name="experts0")
-        nc.scalar.dma_start(experts0[:], w0)
+        half_of_w0 = GROUPS * FEATURES // 2
+        experts0 = [held.tile([FEATURES, half_of_w0], BF16, name=f"experts0_{half}") for half in range(2)]
+        for half, tile in enumerate(experts0):
+            nc.scalar.dma_start(tile[:], w0[:, half * half_of_w0 : (half + 1) * half_of_w0])
         experts1 = held.tile([FEATURES, GROUPS * FEATURES], BF16, name="experts1")
-        nc.scalar.dma_start(experts1[:], w1)
+        nc.sync.dma_start(experts1[:], w1)
 
         zeros = held.tile([FEATURES, BANK], BF16, name="zeros")
         nc.vector.memset(zeros[:], 0.0)
@@ -71,7 +78,7 @@ def tile_newmoe_kernel(tc, table, w0, w1, offs, out):
             for r, e in enumerate(experts_of(p)):
                 nc.tensor.matmul(
                     total[:],
-                    experts0[:, e * FEATURES : (e + 1) * FEATURES],
+                    expert_of(experts0, e),
                     window[:].indirect(offsets[:, p * OFFSET_COLUMNS : (p + 1) * OFFSET_COLUMNS]),
                     start=(r == 0),
                     stop=(r == EXPERTS_OF_A_GROUP - 1),

@@ -64,7 +64,7 @@ def tile_newmoe_kernel(tc, table, w0, w1, offs, out):
         for half, tile in enumerate(experts0):
             nc.scalar.dma_start(tile[:], w0[:, half * half_of_w0 : (half + 1) * half_of_w0])
         experts1 = held.tile([FEATURES, GROUPS * FEATURES], BF16, name="experts1")
-        nc.sync.dma_start(experts1[:], w1)
+        nc.scalar.dma_start(experts1[:], w1)
 
         zeros = held.tile([FEATURES, BANK], BF16, name="zeros")
         nc.vector.memset(zeros[:], 0.0)
@@ -107,4 +107,5 @@ def tile_newmoe_kernel(tc, table, w0, w1, offs, out):
             if p == 1:
                 nc.sync.dma_start(out[:, 0 : 2 * GROUP], first_two[:])
             elif p > 1:
-                nc.sync.dma_start(out[:, p * GROUP : (p + 1) * GROUP], result)
+                queue = nc.sync if p == GROUPS - 1 else nc.scalar
+                queue.dma_start(out[:, p * GROUP : (p + 1) * GROUP], result)

import concourse.mybir as mybir

BF16, F32, U16 = mybir.dt.bfloat16, mybir.dt.float32, mybir.dt.uint16
MULT, MAX = mybir.AluOpType.mult, mybir.AluOpType.max
COPY = mybir.ActivationFunctionType.Copy

FEATURES = 128
SAMPLES = 1024
PICKED = 512
GROUPS = 4
GROUP = PICKED // GROUPS
EXPERTS_OF_A_GROUP = 2
OFFSET_COLUMNS = GROUP // 16
MEAN = 1.0 / EXPERTS_OF_A_GROUP
SLOPE = 0.01
PSUM_BANKS = 8
BANK = 512
WARM_UP = 3

FLOPS = 2 * (2 * FEATURES * FEATURES * PICKED * EXPERTS_OF_A_GROUP)
BYTES = (
    FEATURES * PICKED * 2
    + 2 * FEATURES * GROUPS * FEATURES * 2
    + PICKED * 2
    + FEATURES * PICKED * 4
)


def mean_then_leaky(nc, pool, result, total, width):
    mean = pool.tile([FEATURES, GROUP], F32, name="mean")
    nc.scalar.activation(mean[:, 0:width], total, COPY, scale=MEAN)
    nc.vector.scalar_tensor_tensor(result, mean[:, 0:width], SLOPE, mean[:, 0:width], MULT, MAX)


def experts_of(p):
    return [(p + r) % GROUPS for r in range(EXPERTS_OF_A_GROUP)]


def expert_of(halves, e):
    half, place = divmod(e, GROUPS // 2)
    return halves[half][:, place * FEATURES : (place + 1) * FEATURES]


def pieces_of(p):
    cuts = 2
    width = GROUP // cuts
    return [(c * width, width) for c in range(cuts)]


def tile_newmoe_kernel(tc, table, w0, w1, offs, out):
    nc = tc.nc
    with (
        tc.tile_pool(name="held", bufs=1) as held,
        tc.tile_pool(name="work", bufs=2 * GROUPS) as work,
        tc.psum_pool(name="unread", bufs=1) as unread,
        tc.psum_pool(name="psum", bufs=PSUM_BANKS - 1) as psum,
    ):
        window = held.tile([FEATURES, SAMPLES], BF16, name="window")
        nc.sync.dma_start(window[:], table)
        offsets = held.tile([FEATURES, PICKED // 16], U16, name="offsets")
        nc.sync.dma_start(offsets[:], offs)
        half_of_w0 = GROUPS * FEATURES // 2
        experts0 = [held.tile([FEATURES, half_of_w0], BF16, name=f"experts0_{half}") for half in range(2)]
        for half, tile in enumerate(experts0):
            nc.scalar.dma_start(tile[:], w0[:, half * half_of_w0 : (half + 1) * half_of_w0])
        experts1 = held.tile([FEATURES, GROUPS * FEATURES], BF16, name="experts1")
        nc.scalar.dma_start(experts1[:], w1)

        zeros = held.tile([FEATURES, BANK], BF16, name="zeros")
        nc.vector.memset(zeros[:], 0.0)
        product = unread.tile([FEATURES, BANK], F32, name="product")
        for i in range(WARM_UP):
            nc.tensor.matmul(product[:], zeros[:, 0:FEATURES], zeros[:], start=True, stop=True)

        hidden = []
        for p in range(GROUPS):
            total = psum.tile([FEATURES, GROUP], F32, name="total")
            for r, e in enumerate(experts_of(p)):
                nc.tensor.matmul(
                    total[:],
                    expert_of(experts0, e),
                    window[:].indirect(offsets[:, p * OFFSET_COLUMNS : (p + 1) * OFFSET_COLUMNS]),
                    start=(r == 0),
                    stop=(r == EXPERTS_OF_A_GROUP - 1),
                )
            hidden.append(work.tile([FEATURES, GROUP], BF16, name="hidden"))
            for first, width in pieces_of(p):
                piece = slice(first, first + width)
                mean_then_leaky(nc, work, hidden[p][:, piece], total[:, piece], width)

        first_two = work.tile([FEATURES, 2 * GROUP], F32, name="first_two")
        results = [first_two[:, 0:GROUP], first_two[:, GROUP : 2 * GROUP]]
        results += [work.tile([FEATURES, GROUP], F32, name="result")[:] for p in range(2, GROUPS)]
        for p, result in enumerate(results):
            for first, width in pieces_of(p):
                piece = slice(first, first + width)
                total = psum.tile([FEATURES, GROUP], F32, name="total")
                for r, e in enumerate(experts_of(p)):
                    nc.tensor.matmul(
                        total[:, 0:width],
                        experts1[:, e * FEATURES : (e + 1) * FEATURES],
                        hidden[p][:, piece],
                        start=(r == 0),
                        stop=(r == EXPERTS_OF_A_GROUP - 1),
                    )
                mean_then_leaky(nc, work, result[:, piece], total[:, 0:width], width)
            if p == 1:
                nc.sync.dma_start(out[:, 0 : 2 * GROUP], first_two[:])
            elif p > 1:
                queue = nc.sync if p == GROUPS - 1 else nc.scalar
                queue.dma_start(out[:, p * GROUP : (p + 1) * GROUP], result)
